import numpy as np
import ml_dtypes


def mxq(x, axis, fmt="e4m3"):
    dtype, down = {"e4m3": (ml_dtypes.float8_e4m3fn, 7), "e5m2": (ml_dtypes.float8_e5m2, 14)}[fmt]
    v = np.moveaxis(np.asarray(x, np.float32).astype(ml_dtypes.bfloat16).astype(np.float64), axis, -1)
    blocks = v.reshape(v.shape[:-1] + (-1, 32))
    amax = np.abs(blocks).max(-1, keepdims=True)
    byte = np.maximum(np.where(amax > 0, np.frexp(amax)[1] - 1 + 127, 0) - down, 1)
    scale = np.exp2(byte - 127.0)
    codes = (blocks / scale).astype(np.float32).astype(dtype).astype(np.float64)
    return np.moveaxis((codes * scale).reshape(v.shape), -1, axis)


WIDE = False


def mx_kscale(k):
    if not WIDE:
        return np.ones(k)
    levels = np.array([10, -10, 5, -5, 0])
    if k % 512:
        return np.exp2(np.random.permutation(np.resize(levels, k // 32))).repeat(32)
    a = np.empty((k // 512, 16))
    for p in range(k // 512):
        a[p, :8] = np.random.permutation(np.resize(levels, 8))
        for g in range(8):
            far = levels[np.abs(levels - a[p, g]) >= 10]
            a[p, g + 8] = far[np.random.randint(len(far))]
    return np.exp2(a.ravel()).repeat(32)


BF16 = ml_dtypes.bfloat16


def bf(x):
    return np.asarray(x, np.float32).astype(BF16)


def f64(x):
    return np.asarray(x).astype(np.float64)


B, L, H, U = 2, 1024, 1024, 1024
R_MIN, R_MAX = 0.9, 0.999


def draw0():
    s, t = mx_kscale(H), mx_kscale(U)
    inputs = np.random.standard_normal((B, L, H)) * s
    Wi = np.random.standard_normal((U, H)) / np.sqrt(H) / s[None, :] * t[:, None]
    bi = np.random.standard_normal(U) * 0.03 * t
    Wo = np.random.standard_normal((H, U)) / np.sqrt(U) / t[None, :]
    bo = np.random.standard_normal(H) * 0.1
    r = np.random.uniform(size=U)
    nu_log = np.log(-0.5 * np.log(r * (R_MAX ** 2 - R_MIN ** 2) + R_MIN ** 2))
    gamma_log = np.log(np.sqrt(1.0 - np.exp(-np.exp(nu_log)) ** 2))
    params_log = np.stack([nu_log, gamma_log])
    return {"inputs": bf(inputs), "Wi": bf(Wi), "bi": bf(bi), "Wo": bf(Wo), "bo": bf(bo), "params_log": bf(params_log)}


def core(inputs, Wi, bi, Wo, bo, params_log):
    u = (mxq(f64(inputs), 2, "e4m3") @ mxq(f64(Wi), 1, "e4m3").T) + f64(bi)
    params = np.exp(f64(params_log))
    nu, gamma = params[0], params[1]

    log2_L = int(np.ceil(np.log2(L)))
    pad_len = 2 ** log2_L - L
    x = np.pad(u, ((0, 0), (0, pad_len), (0, 0))) if pad_len else u
    Lp = 2 ** log2_L

    for i in range(1, log2_L + 1):
        l = 2 ** i
        x = x.reshape(B * Lp // l, l, U)
        x1, x2 = x[:, : l // 2], x[:, l // 2:]
        pos = np.arange(1, l // 2 + 1, dtype=np.float64)
        lambs = np.exp(-pos[:, None] * nu)
        x2 = x2 + lambs * x1[:, -1:]
        x = np.concatenate([x1, x2], axis=1).reshape(B, Lp, U)

    x = x[:, :L] * gamma
    return (mxq(x, 2, "e4m3") @ mxq(f64(Wo), 1, "e4m3").T) + f64(bo)


def e4m3fn_bytes(y):
    return np.clip(np.asarray(y, np.float64), -448.0, 448.0).astype(np.float32).astype(ml_dtypes.float8_e4m3fn).view(np.uint8)


def e4m3fn_values(b):
    return np.asarray(b, np.uint8).view(ml_dtypes.float8_e4m3fn).astype(np.float64)


def setup_inputs():
    d = draw0()
    x0 = np.asarray(d['inputs']).astype(np.float64)
    s = (np.max(np.abs(x0), axis=(0, 1), keepdims=True) / 448.0).astype(np.float32)
    out = {}
    for k, v in d.items():
        if k == 'inputs':
            out['inputs_bytes'] = e4m3fn_bytes(x0 / s.astype(np.float64))
            out['inputs_scale'] = s
        else:
            out[k] = v
    return out


def reference(inputs_bytes, inputs_scale, Wi, bi, Wo, bo, params_log):
    return core(e4m3fn_values(inputs_bytes) * inputs_scale.astype(np.float64), Wi, bi, Wo, bo, params_log)

@@ -1,0 +1,286 @@
+from contextlib import ExitStack
+
+import concourse.mybir as mybir
+from concourse.masks import make_identity
+
+B, L, H, U = 2, 1024, 1024, 1024
+FLOPS = 2 * B * L * H * U * 2
+
+F32 = mybir.dt.float32
+BF16 = mybir.dt.bfloat16
+U32 = mybir.dt.uint32
+U8 = mybir.dt.uint8
+FP8 = mybir.dt.float8_e4m3fn
+FP8X4 = mybir.dt.float8_e4m3fn_x4
+ALU = mybir.AluOpType
+ACT = mybir.ActivationFunctionType
+
+P = 128
+N = 512
+
+
+def tile_slru_kernel(tc, inputs_bytes, inputs_scale, Wi, bi, Wo, bo, params_log, out):
+    nc = tc.nc
+    x_rows = inputs_bytes.rearrange("b l k -> (b l) k").rearrange("(j p) k -> p j k", p=P)
+    out_rows = out.rearrange("b l h -> (b l) h").rearrange("(j p) h -> j p h", p=P)
+    wi_rows = Wi.rearrange("(G m t) k -> G m t k", m=P, t=4)
+    wo_rows = Wo.rearrange("(j p) c -> p j c", p=P)
+
+    with ExitStack() as ctx:
+        keep = ctx.enter_context(tc.tile_pool(name="keep", bufs=1))
+        work = ctx.enter_context(tc.tile_pool(name="work", bufs=1))
+        psum = ctx.enter_context(tc.psum_pool(name="psum", bufs=1))
+        ctx.enter_context(tc.manual_schedule())
+
+        scale_cols = keep.tile([P, 8], F32, name="scale_cols")
+        nc.sync.dma_start(out=scale_cols[:], in_=inputs_scale.rearrange("a b (p c) -> (a b p) c", p=P))
+        logs = keep.tile([P, 4, 4], BF16, name="logs")
+        nc.scalar.dma_start(out=logs[:], in_=params_log.rearrange("r (G p t) -> p (r G) t", p=P, t=4))
+        bi_cols = keep.tile([P, 2, 4], BF16, name="bi_cols")
+        nc.scalar.dma_start(out=bi_cols[:], in_=bi.rearrange("(G p t) -> p G t", p=P, t=4))
+
+        x_tiles = {}
+        wi_tiles = {}
+        wo_tiles = {}
+
+        def load_x(j0, n):
+            t = keep.tile([P, n, H], U8, name="xbytes%d" % j0)
+            nc.sync.dma_start(out=t[:], in_=x_rows[:, j0 : j0 + n, :])
+            for i in range(n):
+                x_tiles[j0 + i] = t[:, i, :]
+
+        def load_wi(j0, n):
+            t = keep.tile([P, n, H], BF16, name="wi%d" % j0)
+            nc.sync.dma_start(out=t[:], in_=wi_rows[j0 // 4][:, j0 % 4 : j0 % 4 + n, :])
+            for i in range(n):
+                wi_tiles[j0 + i] = t[:, i, :]
+
+        def load_wo(j0, n):
+            t = keep.tile([P, n, U], BF16, name="wo%d" % j0)
+            nc.sync.dma_start(out=t[:], in_=wo_rows[:, j0 : j0 + n, :])
+            for i in range(n):
+                wo_tiles[j0 + i] = t[:, i, :]
+
+        load_x(0, 2)
+        load_wi(0, 2)
+        load_x(2, 2)
+        load_wi(2, 2)
+        load_x(4, 4)
+        load_wi(4, 4)
+        load_x(8, 4)
+        load_x(12, 4)
+        load_wo(0, 4)
+        load_wo(4, 4)
+        bo_rows = keep.tile([P, H], BF16, name="bo_rows")
+        nc.sync.dma_start(out=bo_rows[:], in_=bo.partition_broadcast(P))
+
+        ident = keep.tile([P, P], F32, name="ident")
+        make_identity(nc, ident[:])
+        lam_pad = keep.tile([P, P], F32, name="lam_pad")
+        nc.gpsimd.memset(lam_pad[:], 0.0)
+
+        def turn_bank():
+            return psum.tile([P, 4, P], F32, name="turn", tag="turn", bufs=3)
+
+        def mm_bank():
+            return psum.tile([P, N], F32, name="mm", tag="mm", bufs=4)
+
+        scale_rows = keep.tile([P, P, 8], F32, name="scale_rows")
+        for half in range(2):
+            bank = turn_bank()
+            for c in range(4):
+                col = scale_cols[:, 4 * half + c : 4 * half + c + 1]
+                nc.tensor.transpose(bank[:, c, :], col.to_broadcast([P, P]), ident[:])
+            nc.vector.tensor_copy(
+                out=scale_rows[:, :, 4 * half : 4 * half + 4], in_=bank[:].rearrange("q c p -> q p c")
+            )
+        scale_flat = scale_rows[:].rearrange("q p c -> q (p c)")
+
+        nu_gamma = keep.tile([P, 16], F32, name="nu_gamma")
+        nc.scalar.activation(out=nu_gamma[:], in_=logs[:].rearrange("p a t -> p (a t)"), func=ACT.Exp)
+        nc.scalar.activation(out=lam_pad[:, 0:8], in_=nu_gamma[:, 0:8], func=ACT.Exp, scale=-1.0)
+        gamma = nu_gamma[:, 8:16]
+        gamma_bi = keep.tile([P, 8], F32, name="gamma_bi")
+        lam_psum = psum.tile([P, P], F32, name="lam_psum")
+
+        def lam_to_psum():
+            bank = turn_bank()
+            nc.tensor.transpose(bank[:, 0, :], lam_pad[:], ident[:])
+            lam_turned = keep.tile([P, P], F32, name="lam_turned")
+            nc.scalar.copy(out=lam_turned[:], in_=bank[:, 0, :])
+            nc.tensor.transpose(lam_psum[:], lam_turned[:], ident[:])
+
+        def turn(rows, dst):
+            words = rows.bitcast(F32)
+            bank = turn_bank()
+            for g in range(2):
+                for u in range(2):
+                    nc.tensor.transpose(
+                        bank[:, 2 * g + u, :], words[:, 256 * g + u : 256 * (g + 1) : 2], ident[:]
+                    )
+            nc.scalar.copy(out=dst, in_=bank[:].rearrange("p (g u) r -> p g r u", g=2))
+
+        grouped = {}
+        codes = {}
+        scales = {}
+
+        def grouped_tile(key):
+            if key not in grouped:
+                grouped[key] = work.tile([P, 2048], F32, name="grouped", tag="grouped", bufs=4, align_bytes=64)
+            return grouped[key]
+
+        def quantize(key, lo=0, hi=1024):
+            if key not in codes:
+                nm = "%s%d" % key
+                codes[key] = keep.tile([P, 1024], U32, name="codes_" + nm, align_bytes=64)
+                scales[key] = keep.tile([P, 1024], U8, name="scales_" + nm, align_bytes=64)
+            nc.vector.quantize_mx(
+                out=codes[key][:, lo:hi].bitcast(FP8X4),
+                scales=scales[key][:, lo:hi],
+                in_=grouped[key][:, 2 * lo : 2 * hi].bitcast(BF16),
+            )
+
+        def prep_x(j):
+            xs = work.tile([P, H], BF16, name="xs", tag="xs", bufs=3)
+            nc.vector.tensor_tensor(out=xs[:], in0=x_tiles[j].bitcast(FP8), in1=scale_flat, op=ALU.mult)
+            dst = grouped_tile(("x", j // 4))[:].rearrange("p (g r u) -> p g r u", g=2, u=2)
+            turn(xs[:], dst[:, :, P * (j % 4) : P * (j % 4 + 1), :])
+
+        def prep_wi(j):
+            dst = grouped_tile(("wi", j // 4))[:].rearrange("p (t g r u) -> p t g r u", t=4, g=2, u=2)
+            turn(wi_tiles[j], dst[:, j % 4, :, :, :])
+
+        def prep_wo(j):
+            dst = grouped_tile(("wo", j // 4))[:].rearrange("p (g r u) -> p g r u", g=2, u=2)
+            turn(wo_tiles[j], dst[:, :, P * (j % 4) : P * (j % 4 + 1), :])
+
+        def mx(bank, lkey, lcol, rkey, rcol, g):
+            nc.tensor.matmul_mx(
+                out=bank[:],
+                lhsT=codes[lkey][:, lcol : lcol + P].bitcast(FP8X4),
+                lhsT_scale=scales[lkey][:, lcol : lcol + P],
+                rhs=codes[rkey][:, rcol : rcol + N].bitcast(FP8X4),
+                rhs_scale=scales[rkey][:, rcol : rcol + N],
+                start=(g == 0),
+                stop=(g == 1),
+            )
+
+        u_tiles = {}
+
+        def mm1(b, i, half):
+            if (b, i) not in u_tiles:
+                u_tiles[(b, i)] = work.tile([P, L], F32, name="u", tag="u", bufs=4)
+            bank = mm_bank()
+            for g in range(2):
+                mx(bank, ("wi", i // 4), P * (2 * (i % 4) + g), ("x", 2 * b + half), N * g, g)
+            nc.scalar.activation(
+                out=u_tiles[(b, i)][:, N * half : N * (half + 1)],
+                in_=bank[:],
+                func=ACT.Identity,
+                scale=gamma[:, i : i + 1],
+                bias=gamma_bi[:, i : i + 1],
+            )
+
+        pairs = {}
+
+        def scan(b, i):
+            key = (b, i // 4)
+            if key not in pairs:
+                pairs[key] = work.tile([P, 2, L], F32, name="pairs", tag="pairs", bufs=2)
+            t = i % 4
+            nc.vector.tensor_tensor_scan(
+                out=pairs[key][:, t // 2, :].bitcast(BF16)[:, t % 2 : 2 * L : 2],
+                data0=lam_psum[:, i : i + 1].to_broadcast([P, L]),
+                data1=u_tiles[(b, i)][:],
+                initial=0.0,
+                op0=ALU.mult,
+                op1=ALU.add,
+            )
+
+        def weave(b, G, lo=0, hi=1024):
+            dst = grouped_tile(("h", 2 * b + G))[:].rearrange("p (n u) -> p n u", u=2)
+            nc.scalar.copy(out=dst[:, lo:hi, :], in_=pairs[(b, G)][:, :, lo:hi].rearrange("p u n -> p n u"))
+
+        out_tiles = {}
+
+        def mm2(b, j, hh, bank):
+            if (b, j) not in out_tiles:
+                out_tiles[(b, j)] = work.tile([P, H], F32, name="res", tag="res", bufs=4)
+            for G in range(2):
+                mx(bank, ("h", 2 * b + G), P * j, ("wo", hh), N * G, G)
+            res = out_tiles[(b, j)]
+            cols = slice(N * hh, N * (hh + 1))
+            nc.vector.tensor_tensor(out=res[:, cols], in0=bank[:], in1=bo_rows[:, cols], op=ALU.add)
+            if hh == 1:
+                nc.sync.dma_start(out=out_rows[8 * b + j], in_=res[:])
+
+        def mm2_tile(b, j):
+            mm2(b, j, 0, mm_bank())
+            mm2(b, j, 1, mm_bank())
+
+        for j in range(8):
+            prep_x(j)
+            prep_wi(j)
+            if j == 1:
+                lam_to_psum()
+                nc.vector.tensor_tensor(
+                    out=gamma_bi[:], in0=gamma, in1=bi_cols[:].rearrange("p a t -> p (a t)"), op=ALU.mult
+                )
+            if j == 5:
+                quantize(("x", 0))
+            if j == 6:
+                quantize(("wi", 0))
+        prep_x(8)
+        mm1(0, 0, 0)
+        mm1(0, 1, 0)
+        prep_x(9)
+        quantize(("x", 1))
+        mm1(0, 0, 1)
+        mm1(0, 1, 1)
+        quantize(("wi", 1))
+        prep_x(10)
+        prep_x(11)
+
+        for i in range(8):
+            nb, ni = divmod(i + 2, 8)
+            mm1(nb, ni, 0)
+            mm1(nb, ni, 1)
+            scan(0, i)
+            if i < 4:
+                prep_x(12 + i)
+            prep_wo(i)
+            if i == 1:
+                quantize(("x", 2))
+            if i == 3:
+                weave(0, 0)
+            if i == 4:
+                quantize(("x", 3))
+            if i == 5:
+                quantize(("h", 0))
+            if i == 6:
+                quantize(("wo", 0))
+        weave(0, 1)
+
+        for i in range(8):
+            if i + 2 < 8:
+                mm1(1, i + 2, 0)
+                mm1(1, i + 2, 1)
+            scan(1, i)
+            if i == 0:
+                quantize(("wo", 1))
+                quantize(("h", 1))
+            if i == 3:
+                weave(1, 0)
+            if i == 4:
+                quantize(("h", 2))
+            if 1 <= i <= 6:
+                mm2_tile(0, i - 1)
+        weave(1, 1, 0, 512)
+        weave(1, 1, 512, 1024)
+        mm2_tile(0, 6)
+        quantize(("h", 3), 0, 512)
+        mm2_tile(0, 7)
+        quantize(("h", 3), 512, 1024)
+        for j in range(8):
+            mm2(1, j, 0, mm_bank())
+            mm2(1, j, 1, turn_bank()[:].rearrange("p c r -> p (c r)"))

@@ -50,29 +50,28 @@ def tile_slru_kernel(tc, inputs_bytes, inputs_scale, Wi, bi, Wo, bo, params_log,
                 x_tiles[j0 + i] = t[:, i, :]
 
         def load_wi(j0, n):
-            t = keep.tile([P, n, H], BF16, name="wi%d" % j0)
+            t = work.tile([P, n, H], BF16, name="wraw", tag="wraw", bufs=5)
             nc.sync.dma_start(out=t[:], in_=wi_rows[j0 // 4][:, j0 % 4 : j0 % 4 + n, :])
             for i in range(n):
                 wi_tiles[j0 + i] = t[:, i, :]
 
         def load_wo(j0, n):
-            t = keep.tile([P, n, U], BF16, name="wo%d" % j0)
+            t = work.tile([P, n, U], BF16, name="wraw", tag="wraw", bufs=5)
             nc.sync.dma_start(out=t[:], in_=wo_rows[:, j0 : j0 + n, :])
             for i in range(n):
                 wo_tiles[j0 + i] = t[:, i, :]
 
-        load_x(0, 2)
         load_wi(0, 2)
-        load_x(2, 2)
+        load_x(0, 2)
         load_wi(2, 2)
+        load_x(2, 2)
         load_x(4, 4)
-        load_wi(4, 4)
+        load_wi(4, 2)
+        load_wi(6, 2)
         load_x(8, 4)
         load_x(12, 4)
-        load_wo(0, 4)
-        load_wo(4, 4)
+        load_wo(0, 2)
         bo_rows = keep.tile([P, H], BF16, name="bo_rows")
-        nc.sync.dma_start(out=bo_rows[:], in_=bo.partition_broadcast(P))
 
         ident = keep.tile([P, P], F32, name="ident")
         make_identity(nc, ident[:])
@@ -81,6 +80,9 @@ def tile_slru_kernel(tc, inputs_bytes, inputs_scale, Wi, bi, Wo, bo, params_log,
 
         def turn_bank():
             return psum.tile([P, 4, P], F32, name="turn", tag="turn", bufs=3)
+
+        def flat_turn_bank():
+            return psum.tile([P, N], F32, name="turn", tag="turn", bufs=3)
 
         def mm_bank():
             return psum.tile([P, N], F32, name="mm", tag="mm", bufs=4)
@@ -91,9 +93,8 @@ def tile_slru_kernel(tc, inputs_bytes, inputs_scale, Wi, bi, Wo, bo, params_log,
             for c in range(4):
                 col = scale_cols[:, 4 * half + c : 4 * half + c + 1]
                 nc.tensor.transpose(bank[:, c, :], col.to_broadcast([P, P]), ident[:])
-            nc.vector.tensor_copy(
-                out=scale_rows[:, :, 4 * half : 4 * half + 4], in_=bank[:].rearrange("q c p -> q p c")
-            )
+            spread = nc.vector.tensor_copy if half == 0 else nc.scalar.copy
+            spread(out=scale_rows[:, :, 4 * half : 4 * half + 4], in_=bank[:].rearrange("q c p -> q p c"))
         scale_flat = scale_rows[:].rearrange("q p c -> q (p c)")
 
         nu_gamma = keep.tile([P, 16], F32, name="nu_gamma")
@@ -103,11 +104,14 @@ def tile_slru_kernel(tc, inputs_bytes, inputs_scale, Wi, bi, Wo, bo, params_log,
         gamma_bi = keep.tile([P, 8], F32, name="gamma_bi")
         lam_psum = psum.tile([P, P], F32, name="lam_psum")
 
-        def lam_to_psum():
+        lam_turned = keep.tile([P, P], F32, name="lam_turned")
+
+        def lam_turn():
             bank = turn_bank()
             nc.tensor.transpose(bank[:, 0, :], lam_pad[:], ident[:])
-            lam_turned = keep.tile([P, P], F32, name="lam_turned")
             nc.scalar.copy(out=lam_turned[:], in_=bank[:, 0, :])
+
+        def lam_back():
             nc.tensor.transpose(lam_psum[:], lam_turned[:], ident[:])
 
         def turn(rows, dst):
@@ -132,17 +136,42 @@ def tile_slru_kernel(tc, inputs_bytes, inputs_scale, Wi, bi, Wo, bo, params_log,
         def quantize(key, lo=0, hi=1024):
             if key not in codes:
                 nm = "%s%d" % key
-                codes[key] = keep.tile([P, 1024], U32, name="codes_" + nm, align_bytes=64)
-                scales[key] = keep.tile([P, 1024], U8, name="scales_" + nm, align_bytes=64)
+                kind = "act" if key[0] in ("x", "h") else "w"
+                depth = 6 if kind == "act" else 4
+                codes[key] = keep.tile([P, 1024], U32, name="codes_" + nm, tag="c" + kind, bufs=depth, align_bytes=64)
+                scales[key] = keep.tile([P, 1024], U8, name="scales_" + nm, tag="s" + kind, bufs=depth, align_bytes=64)
             nc.vector.quantize_mx(
                 out=codes[key][:, lo:hi].bitcast(FP8X4),
                 scales=scales[key][:, lo:hi],
                 in_=grouped[key][:, 2 * lo : 2 * hi].bitcast(BF16),
             )
 
-        def prep_x(j):
+        xs_tiles = {}
+
+        def scale_x(j):
             xs = work.tile([P, H], BF16, name="xs", tag="xs", bufs=3)
+            xs_tiles[j] = xs
             nc.vector.tensor_tensor(out=xs[:], in0=x_tiles[j].bitcast(FP8), in1=scale_flat, op=ALU.mult)
+
+        wide_tiles = {}
+
+        def widen_x(j):
+            wide = work.tile([P, H], BF16, name="wide", tag="wide", bufs=4)
+            wide_tiles[j] = wide
+            nc.scalar.copy(out=wide[:], in_=x_tiles[j].bitcast(FP8))
+
+        def scale_x_pool(j):
+            wide = wide_tiles[j]
+            xs = work.tile([P, H], BF16, name="xs", tag="xs", bufs=3)
+            xs_tiles[j] = xs
+            nc.gpsimd.tensor_tensor(out=xs[:], in0=wide[:], in1=scale_flat, op=ALU.mult)
+
+        def prep_x(j):
+            scale_x(j)
+            turn_x(j)
+
+        def turn_x(j):
+            xs = xs_tiles[j]
             dst = grouped_tile(("x", j // 4))[:].rearrange("p (g r u) -> p g r u", g=2, u=2)
             turn(xs[:], dst[:, :, P * (j % 4) : P * (j % 4 + 1), :])
 
@@ -168,13 +197,13 @@ def tile_slru_kernel(tc, inputs_bytes, inputs_scale, Wi, bi, Wo, bo, params_log,
         u_tiles = {}
 
         def mm1(b, i, half):
-            if (b, i) not in u_tiles:
-                u_tiles[(b, i)] = work.tile([P, L], F32, name="u", tag="u", bufs=4)
+            if (b, i // 4) not in u_tiles:
+                u_tiles[(b, i // 4)] = work.tile([P, 4, L], F32, name="u", tag="u", bufs=3)
             bank = mm_bank()
             for g in range(2):
                 mx(bank, ("wi", i // 4), P * (2 * (i % 4) + g), ("x", 2 * b + half), N * g, g)
             nc.scalar.activation(
-                out=u_tiles[(b, i)][:, N * half : N * (half + 1)],
+                out=u_tiles[(b, i // 4)][:, i % 4, N * half : N * (half + 1)],
                 in_=bank[:],
                 func=ACT.Identity,
                 scale=gamma[:, i : i + 1],
@@ -183,18 +212,36 @@ def tile_slru_kernel(tc, inputs_bytes, inputs_scale, Wi, bi, Wo, bo, params_log,
 
         pairs = {}
 
-        def scan(b, i):
+        def scan(b, i, lo=0):
             key = (b, i // 4)
             if key not in pairs:
                 pairs[key] = work.tile([P, 2, L], F32, name="pairs", tag="pairs", bufs=2)
             t = i % 4
             nc.vector.tensor_tensor_scan(
-                out=pairs[key][:, t // 2, :].bitcast(BF16)[:, t % 2 : 2 * L : 2],
-                data0=lam_psum[:, i : i + 1].to_broadcast([P, L]),
-                data1=u_tiles[(b, i)][:],
+                out=pairs[key][:, t // 2, lo:L].bitcast(BF16)[:, t % 2 : 2 * (L - lo) : 2],
+                data0=lam_psum[:, i : i + 1].to_broadcast([P, L - lo]),
+                data1=u_tiles[key][:, t, lo:L],
                 initial=0.0,
                 op0=ALU.mult,
                 op1=ALU.add,
+            )
+
+        def scan_keep(b, i, hi):
+            row = u_tiles[(b, i // 4)][:, i % 4, 0:hi]
+            nc.vector.tensor_tensor_scan(
+                out=row,
+                data0=lam_psum[:, i : i + 1].to_broadcast([P, hi]),
+                data1=row,
+                initial=0.0,
+                op0=ALU.mult,
+                op1=ALU.add,
+            )
+
+        def weave_round(b, G, lo, hi):
+            dst = grouped_tile(("h", 2 * b + G))[:, 2 * lo : 2 * hi].bitcast(BF16)
+            nc.scalar.copy(
+                out=dst.rearrange("p (c i t) -> p c t i", i=4, t=4),
+                in_=u_tiles[(b, G)][:, :, lo:hi].rearrange("p t (c i) -> p c t i", i=4),
             )
 
         def weave(b, G, lo=0, hi=1024):
@@ -203,84 +250,170 @@ def tile_slru_kernel(tc, inputs_bytes, inputs_scale, Wi, bi, Wo, bo, params_log,
 
         out_tiles = {}
 
-        def mm2(b, j, hh, bank):
-            if (b, j) not in out_tiles:
-                out_tiles[(b, j)] = work.tile([P, H], F32, name="res", tag="res", bufs=4)
-            for G in range(2):
-                mx(bank, ("h", 2 * b + G), P * j, ("wo", hh), N * G, G)
-            res = out_tiles[(b, j)]
-            cols = slice(N * hh, N * (hh + 1))
-            nc.vector.tensor_tensor(out=res[:, cols], in0=bank[:], in1=bo_rows[:, cols], op=ALU.add)
-            if hh == 1:
+        open_banks = {}
+
+        def mm2_tail(j):
+            mm2_vector_open(1, j, mm_bank)
+            mm2_vector_close(1, j)
+
+        def mm2_vector_open(b, j, new_bank=flat_turn_bank):
+            for hh in range(2):
+                bank = new_bank()
+                for G in range(2):
+                    mx(bank, ("h", 2 * b + G), P * j, ("wo", hh), N * G, G)
+                open_banks[(b, j, hh)] = bank
+
+        def mm2_vector_close(b, j):
+            res = work.tile([P, H], F32, name="res", tag="res", bufs=7)
+            for hh in range(2):
+                cols = slice(N * hh, N * (hh + 1))
+                nc.vector.tensor_tensor(
+                    out=res[:, cols], in0=open_banks[(b, j, hh)][:], in1=bo_rows[:, cols], op=ALU.add
+                )
+                if (b, j) == (1, 7):
+                    nc.sync.dma_start(out=out_rows[8 * b + j][:, cols], in_=res[:, cols])
+            if (b, j) != (1, 7):
                 nc.sync.dma_start(out=out_rows[8 * b + j], in_=res[:])
 
-        def mm2_tile(b, j):
-            mm2(b, j, 0, mm_bank())
-            mm2(b, j, 1, mm_bank())
+        def mm2_pool(b, j):
+            res = work.tile([P, H], F32, name="res", tag="res", bufs=7)
+            for hh in range(2):
+                bank = mm_bank()
+                for G in range(2):
+                    mx(bank, ("h", 2 * b + G), P * j, ("wo", hh), N * G, G)
+                nc.scalar.copy(out=res[:, N * hh : N * (hh + 1)], in_=bank[:])
+            nc.gpsimd.tensor_tensor(out=res[:], in0=res[:], in1=bo_rows[:], op=ALU.add)
+            out_tiles[(b, j)] = res
 
+        def store(b, j):
+            nc.sync.dma_start(out=out_rows[8 * b + j], in_=out_tiles[(b, j)][:])
+
+        def mm2_vector(b, j):
+            mm2_vector_open(b, j)
+            mm2_vector_close(b, j)
+
+        prep_wi(0)
+        prep_wi(1)
         for j in range(8):
             prep_x(j)
-            prep_wi(j)
-            if j == 1:
-                lam_to_psum()
+            if j < 6:
+                prep_wi(j + 2)
+            if j == 0:
                 nc.vector.tensor_tensor(
                     out=gamma_bi[:], in0=gamma, in1=bi_cols[:].rearrange("p a t -> p (a t)"), op=ALU.mult
                 )
+                lam_turn()
+            if j == 2:
+                lam_back()
+            if j in (1, 3, 5):
+                load_wo(j + 1, 2)
+            if j == 3:
+                quantize(("wi", 0))
+                widen_x(12)
             if j == 5:
                 quantize(("x", 0))
+                widen_x(13)
             if j == 6:
-                quantize(("wi", 0))
+                mm1(0, 0, 0)
+                mm1(0, 1, 0)
+        nc.sync.dma_start(out=bo_rows[:], in_=bo.partition_broadcast(P))
         prep_x(8)
-        mm1(0, 0, 0)
-        mm1(0, 1, 0)
-        prep_x(9)
-        quantize(("x", 1))
-        mm1(0, 0, 1)
-        mm1(0, 1, 1)
         quantize(("wi", 1))
+        quantize(("x", 1))
+        widen_x(14)
+        mm1(0, 2, 0)
+        mm1(0, 0, 1)
+        widen_x(15)
+        prep_x(9)
+        mm1(0, 1, 1)
         prep_x(10)
+        mm1(0, 2, 1)
         prep_x(11)
 
         for i in range(8):
-            nb, ni = divmod(i + 2, 8)
-            mm1(nb, ni, 0)
-            mm1(nb, ni, 1)
-            scan(0, i)
             if i < 4:
-                prep_x(12 + i)
-            prep_wo(i)
-            if i == 1:
+                scale_x_pool(12 + i)
+            scan(0, i)
+            if i < 5:
+                mm1(0, i + 3, 0)
+                mm1(0, i + 3, 1)
+            if 1 <= i <= 4:
+                turn_x(11 + i)
+            if i < 7:
+                prep_wo(i)
+            if i == 4:
                 quantize(("x", 2))
-            if i == 3:
                 weave(0, 0)
-            if i == 4:
-                quantize(("x", 3))
             if i == 5:
-                quantize(("h", 0))
-            if i == 6:
+                quantize(("x", 3))
+                mm1(1, 0, 0)
+                mm1(1, 1, 0)
                 quantize(("wo", 0))
-        weave(0, 1)
+            if i == 6:
+                prep_wo(7)
+                for k in range(2, 8):
+                    mm1(1, k, 0)
+                quantize(("h", 0))
+        weave(0, 1, 0, 512)
+        weave(0, 1, 512, 1024)
+        quantize(("wo", 1))
+        A = 512
+        scan_keep(1, 0, A)
+        quantize(("h", 1), 0, 512)
+        mm2_pool(0, 0)
+        mm2_pool(0, 1)
+        scan_keep(1, 1, A)
+        quantize(("h", 1), 512, 1024)
 
-        for i in range(8):
-            if i + 2 < 8:
-                mm1(1, i + 2, 0)
-                mm1(1, i + 2, 1)
-            scan(1, i)
-            if i == 0:
-                quantize(("wo", 1))
-                quantize(("h", 1))
+        mm2_vector_open(0, 6)
+        mm1(1, 0, 1)
+        mm1(1, 1, 1)
+        for i in range(2, 8):
+            scan_keep(1, i, A)
+            if i == 2:
+                mm2_pool(0, 2)
+                store(0, 0)
             if i == 3:
-                weave(1, 0)
+                mm2_vector_close(0, 6)
+                weave_round(1, 0, 0, A)
+                mm2_vector_open(0, 7)
+                mm2_pool(0, 3)
+                store(0, 1)
+            if i == 5:
+                mm1(1, 2, 1)
+                mm2_pool(0, 4)
+                store(0, 2)
+                mm1(1, 3, 1)
+                mm1(1, 4, 1)
+        weave_round(1, 1, 0, A)
+        store(0, 3)
+        mm2_pool(0, 5)
+        mm1(1, 5, 1)
+        mm1(1, 6, 1)
+        mm1(1, 7, 1)
+        for i in range(8):
+            scan(1, i, A - 1)
+            if i == 2:
+                mm2_vector_close(0, 7)
+                store(0, 4)
+                quantize(("h", 2), 0, A)
+                quantize(("h", 3), 0, A)
+                mm2_pool(1, 0)
+                mm2_vector_open(1, 2)
+            if i == 3:
+                weave(1, 0, A, L)
+                mm2_pool(1, 1)
+                store(0, 5)
             if i == 4:
-                quantize(("h", 2))
-            if 1 <= i <= 6:
-                mm2_tile(0, i - 1)
-        weave(1, 1, 0, 512)
-        weave(1, 1, 512, 1024)
-        mm2_tile(0, 6)
-        quantize(("h", 3), 0, 512)
-        mm2_tile(0, 7)
-        quantize(("h", 3), 512, 1024)
-        for j in range(8):
-            mm2(1, j, 0, mm_bank())
-            mm2(1, j, 1, turn_bank()[:].rearrange("p c r -> p (c r)"))
+                mm2_vector_close(1, 2)
+                mm2_vector_open(1, 3)
+                store(1, 0)
+        weave(1, 1, A, 768)
+        weave(1, 1, 768, L)
+        mm2_vector_close(1, 3)
+        store(1, 1)
+        quantize(("h", 2), A, L)
+        quantize(("h", 3), A, 768)
+        quantize(("h", 3), 768, L)
+        for j in range(4, 8):
+            mm2_tail(j)

@@ -32,8 +32,8 @@ def tile_slru_kernel(tc, inputs_bytes, inputs_scale, Wi, bi, Wo, bo, params_log,
         psum = ctx.enter_context(tc.psum_pool(name="psum", bufs=1))
         ctx.enter_context(tc.manual_schedule())
 
-        scale_cols = keep.tile([P, 8], F32, name="scale_cols")
-        nc.sync.dma_start(out=scale_cols[:], in_=inputs_scale.rearrange("a b (p c) -> (a b p) c", p=P))
+        scale_cols = keep.tile([P, 2, 4], F32, name="scale_cols")
+        nc.sync.dma_start(out=scale_cols[:], in_=inputs_scale.rearrange("a b (g p c) -> p (a b g) c", p=P, c=4))
         logs = keep.tile([P, 4, 4], BF16, name="logs")
         nc.scalar.dma_start(out=logs[:], in_=params_log.rearrange("r (G p t) -> p (r G) t", p=P, t=4))
         bi_cols = keep.tile([P, 2, 4], BF16, name="bi_cols")
@@ -87,15 +87,15 @@ def tile_slru_kernel(tc, inputs_bytes, inputs_scale, Wi, bi, Wo, bo, params_log,
         def mm_bank():
             return psum.tile([P, N], F32, name="mm", tag="mm", bufs=4)
 
-        scale_rows = keep.tile([P, P, 8], F32, name="scale_rows")
+        scale_rows = keep.tile([P, 2, P, 4], F32, name="scale_rows")
         for half in range(2):
             bank = turn_bank()
             for c in range(4):
-                col = scale_cols[:, 4 * half + c : 4 * half + c + 1]
+                col = scale_cols[:, half, c : c + 1]
                 nc.tensor.transpose(bank[:, c, :], col.to_broadcast([P, P]), ident[:])
             spread = nc.vector.tensor_copy if half == 0 else nc.scalar.copy
-            spread(out=scale_rows[:, :, 4 * half : 4 * half + 4], in_=bank[:].rearrange("q c p -> q p c"))
-        scale_flat = scale_rows[:].rearrange("q p c -> q (p c)")
+            spread(out=scale_rows[:, half, :, :], in_=bank[:].rearrange("q c p -> q p c"))
+        scale_flat = scale_rows[:].rearrange("q g p c -> q (g p c)")
 
         nu_gamma = keep.tile([P, 16], F32, name="nu_gamma")
         nc.scalar.activation(out=nu_gamma[:], in_=logs[:].rearrange("p a t -> p (a t)"), func=ACT.Exp)
@@ -137,7 +137,7 @@ def tile_slru_kernel(tc, inputs_bytes, inputs_scale, Wi, bi, Wo, bo, params_log,
             if key not in codes:
                 nm = "%s%d" % key
                 kind = "act" if key[0] in ("x", "h") else "w"
-                depth = 6 if kind == "act" else 4
+                depth = 5 if kind == "act" else 4
                 codes[key] = keep.tile([P, 1024], U32, name="codes_" + nm, tag="c" + kind, bufs=depth, align_bytes=64)
                 scales[key] = keep.tile([P, 1024], U8, name="scales_" + nm, tag="s" + kind, bufs=depth, align_bytes=64)
             nc.vector.quantize_mx(
@@ -149,22 +149,30 @@ def tile_slru_kernel(tc, inputs_bytes, inputs_scale, Wi, bi, Wo, bo, params_log,
         xs_tiles = {}
 
         def scale_x(j):
-            xs = work.tile([P, H], BF16, name="xs", tag="xs", bufs=3)
+            if j == 10:
+                xs = work.tile([P, H], BF16, name="wide", tag="wide", bufs=1)
+            else:
+                xs = work.tile([P, H], BF16, name="xs", tag="xs", bufs=5)
             xs_tiles[j] = xs
-            nc.vector.tensor_tensor(out=xs[:], in0=x_tiles[j].bitcast(FP8), in1=scale_flat, op=ALU.mult)
+            for cols in [slice(0, N), slice(N, H)] if j == 0 else [slice(0, H)]:
+                nc.vector.tensor_tensor(
+                    out=xs[:, cols], in0=x_tiles[j][:, cols].bitcast(FP8), in1=scale_flat[:, cols], op=ALU.mult
+                )
 
         wide_tiles = {}
 
         def widen_x(j):
-            wide = work.tile([P, H], BF16, name="wide", tag="wide", bufs=4)
+            wide = work.tile([P, H], BF16, name="cast", tag="cast", bufs=4)
             wide_tiles[j] = wide
             nc.scalar.copy(out=wide[:], in_=x_tiles[j].bitcast(FP8))
 
         def scale_x_pool(j):
-            wide = wide_tiles[j]
-            xs = work.tile([P, H], BF16, name="xs", tag="xs", bufs=3)
+            if j == 12:
+                xs = work.tile([P, H], BF16, name="wide", tag="wide", bufs=1)
+            else:
+                xs = work.tile([P, H], BF16, name="xs", tag="xs", bufs=5)
             xs_tiles[j] = xs
-            nc.gpsimd.tensor_tensor(out=xs[:], in0=wide[:], in1=scale_flat, op=ALU.mult)
+            nc.gpsimd.tensor_tensor(out=xs[:], in0=wide_tiles[j][:], in1=scale_flat, op=ALU.mult)
 
         def prep_x(j):
             scale_x(j)
@@ -196,10 +204,10 @@ def tile_slru_kernel(tc, inputs_bytes, inputs_scale, Wi, bi, Wo, bo, params_log,
 
         u_tiles = {}
 
-        def mm1(b, i, half):
+        def mm1(b, i, half, new_bank=mm_bank):
             if (b, i // 4) not in u_tiles:
                 u_tiles[(b, i // 4)] = work.tile([P, 4, L], F32, name="u", tag="u", bufs=3)
-            bank = mm_bank()
+            bank = new_bank()
             for g in range(2):
                 mx(bank, ("wi", i // 4), P * (2 * (i % 4) + g), ("x", 2 * b + half), N * g, g)
             nc.scalar.activation(
@@ -237,34 +245,51 @@ def tile_slru_kernel(tc, inputs_bytes, inputs_scale, Wi, bi, Wo, bo, params_log,
                 op1=ALU.add,
             )
 
-        def weave_round(b, G, lo, hi):
-            dst = grouped_tile(("h", 2 * b + G))[:, 2 * lo : 2 * hi].bitcast(BF16)
+        def weave_round(G):
+            dst = grouped_tile(("h", 2))[:, 1024 * G : 1024 * (G + 1)].bitcast(BF16)
             nc.scalar.copy(
                 out=dst.rearrange("p (c i t) -> p c t i", i=4, t=4),
-                in_=u_tiles[(b, G)][:, :, lo:hi].rearrange("p t (c i) -> p c t i", i=4),
+                in_=u_tiles[(1, G)][:, :, 0:N].rearrange("p t (c i) -> p c t i", i=4),
             )
 
-        def weave(b, G, lo=0, hi=1024):
-            dst = grouped_tile(("h", 2 * b + G))[:].rearrange("p (n u) -> p n u", u=2)
-            nc.scalar.copy(out=dst[:, lo:hi, :], in_=pairs[(b, G)][:, :, lo:hi].rearrange("p u n -> p n u"))
+        def weave(b, G, lo=0, hi=1024, copy=nc.scalar.copy):
+            if b == 0:
+                dst = grouped_tile(("h", G))[:, 2 * lo : 2 * hi]
+            else:
+                dst = grouped_tile(("h", 3))[:, 2 * (N * G + lo - N) : 2 * (N * G + hi - N)]
+            copy(out=dst.rearrange("p (n u) -> p n u", u=2), in_=pairs[(b, G)][:, :, lo:hi].rearrange("p u n -> p n u"))
+
+        def weave_pool(G):
+            dst = grouped_tile(("h", G))[:].bitcast(BF16).rearrange("p (n u e) -> p n u e", u=2, e=2)
+            src = pairs[(0, G)][:].bitcast(BF16).rearrange("p u (n e) -> p n u e", e=2)
+            nc.gpsimd.tensor_scalar(out=dst, in0=src, scalar1=1.0, scalar2=0.0, op0=ALU.mult, op1=ALU.add)
+
+        def h_cols(b, j, G):
+            if b == 0:
+                return ("h", G), P * j
+            return ("h", 2 + j // 4), N * G + P * (j % 4)
 
         out_tiles = {}
 
         open_banks = {}
 
-        def mm2_tail(j):
-            mm2_vector_open(1, j, mm_bank)
-            mm2_vector_close(1, j)
-
-        def mm2_vector_open(b, j, new_bank=flat_turn_bank):
+        def mm2(b, j, G, new_bank=None):
             for hh in range(2):
-                bank = new_bank()
-                for G in range(2):
-                    mx(bank, ("h", 2 * b + G), P * j, ("wo", hh), N * G, G)
-                open_banks[(b, j, hh)] = bank
+                if G == 0:
+                    open_banks[(b, j, hh)] = new_bank()
+                key, col = h_cols(b, j, G)
+                mx(open_banks[(b, j, hh)], key, col, ("wo", hh), N * G, G)
 
-        def mm2_vector_close(b, j):
+        def mm2_both(b, j, new_bank):
+            mm2(b, j, 0, new_bank)
+            mm2(b, j, 1)
+
+        def store(b, j):
+            nc.sync.dma_start(out=out_rows[8 * b + j], in_=out_tiles[(b, j)][:])
+
+        def finish_vector(b, j):
             res = work.tile([P, H], F32, name="res", tag="res", bufs=7)
+            out_tiles[(b, j)] = res
             for hh in range(2):
                 cols = slice(N * hh, N * (hh + 1))
                 nc.vector.tensor_tensor(
@@ -273,29 +298,35 @@ def tile_slru_kernel(tc, inputs_bytes, inputs_scale, Wi, bi, Wo, bo, params_log,
                 if (b, j) == (1, 7):
                     nc.sync.dma_start(out=out_rows[8 * b + j][:, cols], in_=res[:, cols])
             if (b, j) != (1, 7):
-                nc.sync.dma_start(out=out_rows[8 * b + j], in_=res[:])
+                store(b, j)
 
-        def mm2_pool(b, j):
+        def finish_pool(b, j):
             res = work.tile([P, H], F32, name="res", tag="res", bufs=7)
-            for hh in range(2):
-                bank = mm_bank()
-                for G in range(2):
-                    mx(bank, ("h", 2 * b + G), P * j, ("wo", hh), N * G, G)
-                nc.scalar.copy(out=res[:, N * hh : N * (hh + 1)], in_=bank[:])
-            nc.gpsimd.tensor_tensor(out=res[:], in0=res[:], in1=bo_rows[:], op=ALU.add)
             out_tiles[(b, j)] = res
-
-        def store(b, j):
-            nc.sync.dma_start(out=out_rows[8 * b + j], in_=out_tiles[(b, j)][:])
-
-        def mm2_vector(b, j):
-            mm2_vector_open(b, j)
-            mm2_vector_close(b, j)
+            for hh in range(2):
+                nc.scalar.copy(out=res[:, N * hh : N * (hh + 1)], in_=open_banks[(b, j, hh)][:])
+            nc.gpsimd.tensor_tensor(out=res[:], in0=res[:], in1=bo_rows[:], op=ALU.add)
 
         prep_wi(0)
         prep_wi(1)
-        for j in range(8):
-            prep_x(j)
+        for j in range(12):
+            scale_x(j)
+            if j == 4:
+                quantize(("wi", 0))
+            if j == 6:
+                quantize(("x", 0))
+            if j == 8:
+                quantize(("wi", 1))
+            if j == 9:
+                quantize(("x", 1))
+            if j == 7:
+                mm1(0, 0, 0)
+                mm1(0, 1, 0)
+            if j == 9:
+                mm1(0, 2, 0)
+            if j >= 10:
+                mm1(0, j - 10, 1)
+            turn_x(j)
             if j < 6:
                 prep_wi(j + 2)
             if j == 0:
@@ -307,28 +338,12 @@ def tile_slru_kernel(tc, inputs_bytes, inputs_scale, Wi, bi, Wo, bo, params_log,
                 lam_back()
             if j in (1, 3, 5):
                 load_wo(j + 1, 2)
-            if j == 3:
-                quantize(("wi", 0))
-                widen_x(12)
-            if j == 5:
-                quantize(("x", 0))
-                widen_x(13)
-            if j == 6:
-                mm1(0, 0, 0)
-                mm1(0, 1, 0)
-        nc.sync.dma_start(out=bo_rows[:], in_=bo.partition_broadcast(P))
-        prep_x(8)
-        quantize(("wi", 1))
-        quantize(("x", 1))
-        widen_x(14)
-        mm1(0, 2, 0)
-        mm1(0, 0, 1)
-        widen_x(15)
-        prep_x(9)
-        mm1(0, 1, 1)
-        prep_x(10)
-        mm1(0, 2, 1)
-        prep_x(11)
+            if j == 7:
+                nc.sync.dma_start(out=bo_rows[:], in_=bo.partition_broadcast(P))
+            if j in (5, 7, 10, 11):
+                widen_x(12 + (5, 7, 10, 11).index(j)) if (5, 7, 10, 11).index(j) < 4 else None
+        for k in range(12 - 10, 3):
+            mm1(0, k, 1)
 
         for i in range(8):
             if i < 4:
@@ -337,83 +352,105 @@ def tile_slru_kernel(tc, inputs_bytes, inputs_scale, Wi, bi, Wo, bo, params_log,
             if i < 5:
                 mm1(0, i + 3, 0)
                 mm1(0, i + 3, 1)
-            if 1 <= i <= 4:
-                turn_x(11 + i)
-            if i < 7:
+            if i in (1,2,3,4):
+                turn_x(12 + (1,2,3,4).index(i))
+            if i < 6:
                 prep_wo(i)
-            if i == 4:
+            if i in (4, 5):
+                prep_wo(i + 2)
+            if i == 3:
+                weave_pool(0)
+            if i == 6:
                 quantize(("x", 2))
-                weave(0, 0)
-            if i == 5:
-                quantize(("x", 3))
-                mm1(1, 0, 0)
-                mm1(1, 1, 0)
+                for k in range(4):
+                    mm1(1, k, 0)
                 quantize(("wo", 0))
             if i == 6:
-                prep_wo(7)
-                for k in range(2, 8):
-                    mm1(1, k, 0)
+                quantize(("x", 3))
                 quantize(("h", 0))
+                for k in range(4, 6):
+                    mm1(1, k, 0)
         weave(0, 1, 0, 512)
         weave(0, 1, 512, 1024)
         quantize(("wo", 1))
-        A = 512
-        scan_keep(1, 0, A)
+        mm1(1, 6, 0)
+        mm1(1, 7, 0)
+        mm2(0, 0, 0, mm_bank)
+        scan_keep(1, 0, N)
         quantize(("h", 1), 0, 512)
-        mm2_pool(0, 0)
-        mm2_pool(0, 1)
-        scan_keep(1, 1, A)
+        mm2(0, 0, 1)
+        finish_pool(0, 0)
+        mm2_both(0, 1, mm_bank)
+        finish_pool(0, 1)
+        scan_keep(1, 1, N)
         quantize(("h", 1), 512, 1024)
-
-        mm2_vector_open(0, 6)
+        mm2_both(0, 2, mm_bank)
+        finish_pool(0, 2)
+        mm2_both(0, 6, flat_turn_bank)
+        store(0, 0)
+        for i in range(2, 5):
+            scan_keep(1, i, N)
+            if i == 3:
+                weave_round(0)
+        finish_vector(0, 6)
+        mm2_both(0, 3, mm_bank)
+        finish_pool(0, 3)
+        store(0, 1)
         mm1(1, 0, 1)
         mm1(1, 1, 1)
-        for i in range(2, 8):
-            scan_keep(1, i, A)
-            if i == 2:
-                mm2_pool(0, 2)
-                store(0, 0)
-            if i == 3:
-                mm2_vector_close(0, 6)
-                weave_round(1, 0, 0, A)
-                mm2_vector_open(0, 7)
-                mm2_pool(0, 3)
-                store(0, 1)
-            if i == 5:
-                mm1(1, 2, 1)
-                mm2_pool(0, 4)
-                store(0, 2)
-                mm1(1, 3, 1)
-                mm1(1, 4, 1)
-        weave_round(1, 1, 0, A)
+        mm2_both(0, 7, flat_turn_bank)
+        for i in range(5, 8):
+            scan_keep(1, i, N)
+        weave_round(1)
+        store(0, 2)
+        finish_vector(0, 7)
+        mm2_both(0, 4, mm_bank)
+        finish_pool(0, 4)
+        mm1(1, 2, 1)
+        mm1(1, 3, 1)
+        scan(1, 0, N - 1)
+        scan(1, 1, N - 1)
+        quantize(("h", 2))
         store(0, 3)
-        mm2_pool(0, 5)
+        mm2_both(0, 5, mm_bank)
+        finish_pool(0, 5)
+        mm2_both(1, 2, flat_turn_bank)
+        mm1(1, 4, 1)
         mm1(1, 5, 1)
+        pass
+        scan(1, 2, N - 1)
+        scan(1, 3, N - 1)
+        finish_vector(1, 2)
+        store(0, 4)
+        mm2_both(1, 0, mm_bank)
+        finish_pool(1, 0)
         mm1(1, 6, 1)
         mm1(1, 7, 1)
-        for i in range(8):
-            scan(1, i, A - 1)
-            if i == 2:
-                mm2_vector_close(0, 7)
-                store(0, 4)
-                quantize(("h", 2), 0, A)
-                quantize(("h", 3), 0, A)
-                mm2_pool(1, 0)
-                mm2_vector_open(1, 2)
-            if i == 3:
-                weave(1, 0, A, L)
-                mm2_pool(1, 1)
-                store(0, 5)
-            if i == 4:
-                mm2_vector_close(1, 2)
-                mm2_vector_open(1, 3)
-                store(1, 0)
-        weave(1, 1, A, 768)
+        weave(1, 0, N, L)
+        mm2_both(1, 1, flat_turn_bank)
+        scan(1, 4, N - 1)
+        store(0, 5)
+        scan(1, 5, N - 1)
+        mm2_both(1, 3, mm_bank)
+        scan(1, 6, N - 1)
+        finish_vector(1, 1)
+        quantize(("h", 3), 0, N)
+        mm2(1, 4, 0, mm_bank)
+        store(1, 0)
+        scan(1, 7, N - 1)
+        weave(1, 1, N, 768)
         weave(1, 1, 768, L)
-        mm2_vector_close(1, 3)
-        store(1, 1)
-        quantize(("h", 2), A, L)
-        quantize(("h", 3), A, 768)
+        mm2(1, 5, 0, flat_turn_bank)
+        finish_vector(1, 3)
+        quantize(("h", 3), N, 768)
+        mm2(1, 4, 1)
+        mm2(1, 5, 1)
         quantize(("h", 3), 768, L)
-        for j in range(4, 8):
-            mm2_tail(j)
+        mm2_both(1, 6, mm_bank)
+        pass
+        finish_vector(1, 4)
+        mm2_both(1, 7, mm_bank)
+        finish_vector(1, 5)
+        finish_vector(1, 6)
+        pass
+        finish_vector(1, 7)

from contextlib import ExitStack

import concourse.mybir as mybir
from concourse.masks import make_identity

B, L, H, U = 2, 1024, 1024, 1024
FLOPS = 2 * B * L * H * U * 2

F32 = mybir.dt.float32
BF16 = mybir.dt.bfloat16
U32 = mybir.dt.uint32
U8 = mybir.dt.uint8
FP8 = mybir.dt.float8_e4m3fn
FP8X4 = mybir.dt.float8_e4m3fn_x4
ALU = mybir.AluOpType
ACT = mybir.ActivationFunctionType

P = 128
N = 512


def tile_slru_kernel(tc, inputs_bytes, inputs_scale, Wi, bi, Wo, bo, params_log, out):
    nc = tc.nc
    x_rows = inputs_bytes.rearrange("b l k -> (b l) k").rearrange("(j p) k -> p j k", p=P)
    out_rows = out.rearrange("b l h -> (b l) h").rearrange("(j p) h -> j p h", p=P)
    wi_rows = Wi.rearrange("(G m t) k -> G m t k", m=P, t=4)
    wo_rows = Wo.rearrange("(j p) c -> p j c", p=P)

    with ExitStack() as ctx:
        keep = ctx.enter_context(tc.tile_pool(name="keep", bufs=1))
        work = ctx.enter_context(tc.tile_pool(name="work", bufs=1))
        psum = ctx.enter_context(tc.psum_pool(name="psum", bufs=1))
        ctx.enter_context(tc.manual_schedule())

        scale_cols = keep.tile([P, 2, 4], F32, name="scale_cols")
        nc.sync.dma_start(out=scale_cols[:], in_=inputs_scale.rearrange("a b (g p c) -> p (a b g) c", p=P, c=4))
        logs = keep.tile([P, 4, 4], BF16, name="logs")
        nc.scalar.dma_start(out=logs[:], in_=params_log.rearrange("r (G p t) -> p (r G) t", p=P, t=4))
        bi_cols = keep.tile([P, 2, 4], BF16, name="bi_cols")
        nc.scalar.dma_start(out=bi_cols[:], in_=bi.rearrange("(G p t) -> p G t", p=P, t=4))

        x_tiles = {}
        wi_tiles = {}
        wo_tiles = {}

        def load_x(j0, n):
            t = keep.tile([P, n, H], U8, name="xbytes%d" % j0)
            nc.sync.dma_start(out=t[:], in_=x_rows[:, j0 : j0 + n, :])
            for i in range(n):
                x_tiles[j0 + i] = t[:, i, :]

        def load_wi(j0, n):
            t = work.tile([P, n, H], BF16, name="wraw", tag="wraw", bufs=5)
            nc.sync.dma_start(out=t[:], in_=wi_rows[j0 // 4][:, j0 % 4 : j0 % 4 + n, :])
            for i in range(n):
                wi_tiles[j0 + i] = t[:, i, :]

        def load_wo(j0, n):
            t = work.tile([P, n, U], BF16, name="wraw", tag="wraw", bufs=5)
            nc.sync.dma_start(out=t[:], in_=wo_rows[:, j0 : j0 + n, :])
            for i in range(n):
                wo_tiles[j0 + i] = t[:, i, :]

        load_wi(0, 2)
        load_x(0, 2)
        load_wi(2, 2)
        load_x(2, 2)
        load_x(4, 4)
        load_wi(4, 2)
        load_wi(6, 2)
        load_x(8, 4)
        load_x(12, 4)
        load_wo(0, 2)
        bo_rows = keep.tile([P, H], BF16, name="bo_rows")

        ident = keep.tile([P, P], F32, name="ident")
        make_identity(nc, ident[:])
        lam_pad = keep.tile([P, P], F32, name="lam_pad")
        nc.gpsimd.memset(lam_pad[:], 0.0)

        def turn_bank():
            return psum.tile([P, 4, P], F32, name="turn", tag="turn", bufs=3)

        def flat_turn_bank():
            return psum.tile([P, N], F32, name="turn", tag="turn", bufs=3)

        def mm_bank():
            return psum.tile([P, N], F32, name="mm", tag="mm", bufs=4)

        scale_rows = keep.tile([P, 2, P, 4], F32, name="scale_rows")
        for half in range(2):
            bank = turn_bank()
            for c in range(4):
                col = scale_cols[:, half, c : c + 1]
                nc.tensor.transpose(bank[:, c, :], col.to_broadcast([P, P]), ident[:])
            spread = nc.vector.tensor_copy if half == 0 else nc.scalar.copy
            spread(out=scale_rows[:, half, :, :], in_=bank[:].rearrange("q c p -> q p c"))
        scale_flat = scale_rows[:].rearrange("q g p c -> q (g p c)")

        nu_gamma = keep.tile([P, 16], F32, name="nu_gamma")
        nc.scalar.activation(out=nu_gamma[:], in_=logs[:].rearrange("p a t -> p (a t)"), func=ACT.Exp)
        nc.scalar.activation(out=lam_pad[:, 0:8], in_=nu_gamma[:, 0:8], func=ACT.Exp, scale=-1.0)
        gamma = nu_gamma[:, 8:16]
        gamma_bi = keep.tile([P, 8], F32, name="gamma_bi")
        lam_psum = psum.tile([P, P], F32, name="lam_psum")

        lam_turned = keep.tile([P, P], F32, name="lam_turned")

        def lam_turn():
            bank = turn_bank()
            nc.tensor.transpose(bank[:, 0, :], lam_pad[:], ident[:])
            nc.scalar.copy(out=lam_turned[:], in_=bank[:, 0, :])

        def lam_back():
            nc.tensor.transpose(lam_psum[:], lam_turned[:], ident[:])

        def turn(rows, dst):
            words = rows.bitcast(F32)
            bank = turn_bank()
            for g in range(2):
                for u in range(2):
                    nc.tensor.transpose(
                        bank[:, 2 * g + u, :], words[:, 256 * g + u : 256 * (g + 1) : 2], ident[:]
                    )
            nc.scalar.copy(out=dst, in_=bank[:].rearrange("p (g u) r -> p g r u", g=2))

        grouped = {}
        codes = {}
        scales = {}

        def grouped_tile(key):
            if key not in grouped:
                grouped[key] = work.tile([P, 2048], F32, name="grouped", tag="grouped", bufs=4, align_bytes=64)
            return grouped[key]

        def quantize(key, lo=0, hi=1024):
            if key not in codes:
                nm = "%s%d" % key
                kind = "act" if key[0] in ("x", "h") else "w"
                depth = 5 if kind == "act" else 4
                codes[key] = keep.tile([P, 1024], U32, name="codes_" + nm, tag="c" + kind, bufs=depth, align_bytes=64)
                scales[key] = keep.tile([P, 1024], U8, name="scales_" + nm, tag="s" + kind, bufs=depth, align_bytes=64)
            nc.vector.quantize_mx(
                out=codes[key][:, lo:hi].bitcast(FP8X4),
                scales=scales[key][:, lo:hi],
                in_=grouped[key][:, 2 * lo : 2 * hi].bitcast(BF16),
            )

        xs_tiles = {}

        def scale_x(j):
            if j == 10:
                xs = work.tile([P, H], BF16, name="wide", tag="wide", bufs=1)
            else:
                xs = work.tile([P, H], BF16, name="xs", tag="xs", bufs=5)
            xs_tiles[j] = xs
            for cols in [slice(0, N), slice(N, H)] if j == 0 else [slice(0, H)]:
                nc.vector.tensor_tensor(
                    out=xs[:, cols], in0=x_tiles[j][:, cols].bitcast(FP8), in1=scale_flat[:, cols], op=ALU.mult
                )

        wide_tiles = {}

        def widen_x(j):
            wide = work.tile([P, H], BF16, name="cast", tag="cast", bufs=4)
            wide_tiles[j] = wide
            nc.scalar.copy(out=wide[:], in_=x_tiles[j].bitcast(FP8))

        def scale_x_pool(j):
            if j == 12:
                xs = work.tile([P, H], BF16, name="wide", tag="wide", bufs=1)
            else:
                xs = work.tile([P, H], BF16, name="xs", tag="xs", bufs=5)
            xs_tiles[j] = xs
            nc.gpsimd.tensor_tensor(out=xs[:], in0=wide_tiles[j][:], in1=scale_flat, op=ALU.mult)

        def prep_x(j):
            scale_x(j)
            turn_x(j)

        def turn_x(j):
            xs = xs_tiles[j]
            dst = grouped_tile(("x", j // 4))[:].rearrange("p (g r u) -> p g r u", g=2, u=2)
            turn(xs[:], dst[:, :, P * (j % 4) : P * (j % 4 + 1), :])

        def prep_wi(j):
            dst = grouped_tile(("wi", j // 4))[:].rearrange("p (t g r u) -> p t g r u", t=4, g=2, u=2)
            turn(wi_tiles[j], dst[:, j % 4, :, :, :])

        def prep_wo(j):
            dst = grouped_tile(("wo", j // 4))[:].rearrange("p (g r u) -> p g r u", g=2, u=2)
            turn(wo_tiles[j], dst[:, :, P * (j % 4) : P * (j % 4 + 1), :])

        def mx(bank, lkey, lcol, rkey, rcol, g):
            nc.tensor.matmul_mx(
                out=bank[:],
                lhsT=codes[lkey][:, lcol : lcol + P].bitcast(FP8X4),
                lhsT_scale=scales[lkey][:, lcol : lcol + P],
                rhs=codes[rkey][:, rcol : rcol + N].bitcast(FP8X4),
                rhs_scale=scales[rkey][:, rcol : rcol + N],
                start=(g == 0),
                stop=(g == 1),
            )

        u_tiles = {}

        def mm1(b, i, half, new_bank=mm_bank):
            if (b, i // 4) not in u_tiles:
                u_tiles[(b, i // 4)] = work.tile([P, 4, L], F32, name="u", tag="u", bufs=3)
            bank = new_bank()
            for g in range(2):
                mx(bank, ("wi", i // 4), P * (2 * (i % 4) + g), ("x", 2 * b + half), N * g, g)
            nc.scalar.activation(
                out=u_tiles[(b, i // 4)][:, i % 4, N * half : N * (half + 1)],
                in_=bank[:],
                func=ACT.Identity,
                scale=gamma[:, i : i + 1],
                bias=gamma_bi[:, i : i + 1],
            )

        pairs = {}

        def scan(b, i, lo=0):
            key = (b, i // 4)
            if key not in pairs:
                pairs[key] = work.tile([P, 2, L], F32, name="pairs", tag="pairs", bufs=2)
            t = i % 4
            nc.vector.tensor_tensor_scan(
                out=pairs[key][:, t // 2, lo:L].bitcast(BF16)[:, t % 2 : 2 * (L - lo) : 2],
                data0=lam_psum[:, i : i + 1].to_broadcast([P, L - lo]),
                data1=u_tiles[key][:, t, lo:L],
                initial=0.0,
                op0=ALU.mult,
                op1=ALU.add,
            )

        def scan_keep(b, i, hi):
            row = u_tiles[(b, i // 4)][:, i % 4, 0:hi]
            nc.vector.tensor_tensor_scan(
                out=row,
                data0=lam_psum[:, i : i + 1].to_broadcast([P, hi]),
                data1=row,
                initial=0.0,
                op0=ALU.mult,
                op1=ALU.add,
            )

        def weave_round(G):
            dst = grouped_tile(("h", 2))[:, 1024 * G : 1024 * (G + 1)].bitcast(BF16)
            nc.scalar.copy(
                out=dst.rearrange("p (c i t) -> p c t i", i=4, t=4),
                in_=u_tiles[(1, G)][:, :, 0:N].rearrange("p t (c i) -> p c t i", i=4),
            )

        def weave(b, G, lo=0, hi=1024, copy=nc.scalar.copy):
            if b == 0:
                dst = grouped_tile(("h", G))[:, 2 * lo : 2 * hi]
            else:
                dst = grouped_tile(("h", 3))[:, 2 * (N * G + lo - N) : 2 * (N * G + hi - N)]
            copy(out=dst.rearrange("p (n u) -> p n u", u=2), in_=pairs[(b, G)][:, :, lo:hi].rearrange("p u n -> p n u"))

        def weave_pool(G):
            dst = grouped_tile(("h", G))[:].bitcast(BF16).rearrange("p (n u e) -> p n u e", u=2, e=2)
            src = pairs[(0, G)][:].bitcast(BF16).rearrange("p u (n e) -> p n u e", e=2)
            nc.gpsimd.tensor_scalar(out=dst, in0=src, scalar1=1.0, scalar2=0.0, op0=ALU.mult, op1=ALU.add)

        def h_cols(b, j, G):
            if b == 0:
                return ("h", G), P * j
            return ("h", 2 + j // 4), N * G + P * (j % 4)

        out_tiles = {}

        open_banks = {}

        def mm2(b, j, G, new_bank=None):
            for hh in range(2):
                if G == 0:
                    open_banks[(b, j, hh)] = new_bank()
                key, col = h_cols(b, j, G)
                mx(open_banks[(b, j, hh)], key, col, ("wo", hh), N * G, G)

        def mm2_both(b, j, new_bank):
            mm2(b, j, 0, new_bank)
            mm2(b, j, 1)

        def store(b, j):
            nc.sync.dma_start(out=out_rows[8 * b + j], in_=out_tiles[(b, j)][:])

        def finish_vector(b, j):
            res = work.tile([P, H], F32, name="res", tag="res", bufs=7)
            out_tiles[(b, j)] = res
            for hh in range(2):
                cols = slice(N * hh, N * (hh + 1))
                nc.vector.tensor_tensor(
                    out=res[:, cols], in0=open_banks[(b, j, hh)][:], in1=bo_rows[:, cols], op=ALU.add
                )
                if (b, j) == (1, 7):
                    nc.sync.dma_start(out=out_rows[8 * b + j][:, cols], in_=res[:, cols])
            if (b, j) != (1, 7):
                store(b, j)

        def finish_pool(b, j):
            res = work.tile([P, H], F32, name="res", tag="res", bufs=7)
            out_tiles[(b, j)] = res
            for hh in range(2):
                nc.scalar.copy(out=res[:, N * hh : N * (hh + 1)], in_=open_banks[(b, j, hh)][:])
            nc.gpsimd.tensor_tensor(out=res[:], in0=res[:], in1=bo_rows[:], op=ALU.add)

        prep_wi(0)
        prep_wi(1)
        for j in range(12):
            scale_x(j)
            if j == 4:
                quantize(("wi", 0))
            if j == 6:
                quantize(("x", 0))
            if j == 8:
                quantize(("wi", 1))
            if j == 9:
                quantize(("x", 1))
            if j == 7:
                mm1(0, 0, 0)
                mm1(0, 1, 0)
            if j == 9:
                mm1(0, 2, 0)
            if j >= 10:
                mm1(0, j - 10, 1)
            turn_x(j)
            if j < 6:
                prep_wi(j + 2)
            if j == 0:
                nc.vector.tensor_tensor(
                    out=gamma_bi[:], in0=gamma, in1=bi_cols[:].rearrange("p a t -> p (a t)"), op=ALU.mult
                )
                lam_turn()
            if j == 2:
                lam_back()
            if j in (1, 3, 5):
                load_wo(j + 1, 2)
            if j == 7:
                nc.sync.dma_start(out=bo_rows[:], in_=bo.partition_broadcast(P))
            if j in (5, 7, 10, 11):
                widen_x(12 + (5, 7, 10, 11).index(j)) if (5, 7, 10, 11).index(j) < 4 else None
        for k in range(12 - 10, 3):
            mm1(0, k, 1)

        for i in range(8):
            if i < 4:
                scale_x_pool(12 + i)
            scan(0, i)
            if i < 5:
                mm1(0, i + 3, 0)
                mm1(0, i + 3, 1)
            if i in (1,2,3,4):
                turn_x(12 + (1,2,3,4).index(i))
            if i < 6:
                prep_wo(i)
            if i in (4, 5):
                prep_wo(i + 2)
            if i == 3:
                weave_pool(0)
            if i == 6:
                quantize(("x", 2))
                for k in range(4):
                    mm1(1, k, 0)
                quantize(("wo", 0))
            if i == 6:
                quantize(("x", 3))
                quantize(("h", 0))
                for k in range(4, 6):
                    mm1(1, k, 0)
        weave(0, 1, 0, 512)
        weave(0, 1, 512, 1024)
        quantize(("wo", 1))
        mm1(1, 6, 0)
        mm1(1, 7, 0)
        mm2(0, 0, 0, mm_bank)
        scan_keep(1, 0, N)
        quantize(("h", 1), 0, 512)
        mm2(0, 0, 1)
        finish_pool(0, 0)
        mm2_both(0, 1, mm_bank)
        finish_pool(0, 1)
        scan_keep(1, 1, N)
        quantize(("h", 1), 512, 1024)
        mm2_both(0, 2, mm_bank)
        finish_pool(0, 2)
        mm2_both(0, 6, flat_turn_bank)
        store(0, 0)
        for i in range(2, 5):
            scan_keep(1, i, N)
            if i == 3:
                weave_round(0)
        finish_vector(0, 6)
        mm2_both(0, 3, mm_bank)
        finish_pool(0, 3)
        store(0, 1)
        mm1(1, 0, 1)
        mm1(1, 1, 1)
        mm2_both(0, 7, flat_turn_bank)
        for i in range(5, 8):
            scan_keep(1, i, N)
        weave_round(1)
        store(0, 2)
        finish_vector(0, 7)
        mm2_both(0, 4, mm_bank)
        finish_pool(0, 4)
        mm1(1, 2, 1)
        mm1(1, 3, 1)
        scan(1, 0, N - 1)
        scan(1, 1, N - 1)
        quantize(("h", 2))
        store(0, 3)
        mm2_both(0, 5, mm_bank)
        finish_pool(0, 5)
        mm2_both(1, 2, flat_turn_bank)
        mm1(1, 4, 1)
        mm1(1, 5, 1)
        pass
        scan(1, 2, N - 1)
        scan(1, 3, N - 1)
        finish_vector(1, 2)
        store(0, 4)
        mm2_both(1, 0, mm_bank)
        finish_pool(1, 0)
        mm1(1, 6, 1)
        mm1(1, 7, 1)
        weave(1, 0, N, L)
        mm2_both(1, 1, flat_turn_bank)
        scan(1, 4, N - 1)
        store(0, 5)
        scan(1, 5, N - 1)
        mm2_both(1, 3, mm_bank)
        scan(1, 6, N - 1)
        finish_vector(1, 1)
        quantize(("h", 3), 0, N)
        mm2(1, 4, 0, mm_bank)
        store(1, 0)
        scan(1, 7, N - 1)
        weave(1, 1, N, 768)
        weave(1, 1, 768, L)
        mm2(1, 5, 0, flat_turn_bank)
        finish_vector(1, 3)
        quantize(("h", 3), N, 768)
        mm2(1, 4, 1)
        mm2(1, 5, 1)
        quantize(("h", 3), 768, L)
        mm2_both(1, 6, mm_bank)
        pass
        finish_vector(1, 4)
        mm2_both(1, 7, mm_bank)
        finish_vector(1, 5)
        finish_vector(1, 6)
        pass
        finish_vector(1, 7)
